import numpy as np
import ml_dtypes


def mxq(x, axis, fmt="e4m3"):
    dtype, down = {"e4m3": (ml_dtypes.float8_e4m3fn, 7), "e5m2": (ml_dtypes.float8_e5m2, 14)}[fmt]
    v = np.moveaxis(np.asarray(x, np.float32).astype(ml_dtypes.bfloat16).astype(np.float64), axis, -1)
    blocks = v.reshape(v.shape[:-1] + (-1, 32))
    amax = np.abs(blocks).max(-1, keepdims=True)
    byte = np.maximum(np.where(amax > 0, np.frexp(amax)[1] - 1 + 127, 0) - down, 1)
    scale = np.exp2(byte - 127.0)
    codes = (blocks / scale).astype(np.float32).astype(dtype).astype(np.float64)
    return np.moveaxis((codes * scale).reshape(v.shape), -1, axis)


WIDE = False


def mx_kscale(k):
    if not WIDE:
        return np.ones(k)
    levels = np.array([10, -10, 5, -5, 0])
    a = np.random.permutation(np.resize(levels, k // 512 * 4)).reshape(k // 512, 4)
    idx = np.arange(k)
    return np.exp2(a[idx // 512, idx % 128 // 32])


BF16 = ml_dtypes.bfloat16


def bf(x):
    return np.asarray(x, np.float32).astype(BF16)


def f64(x):
    return np.asarray(x).astype(np.float64)


E2M1 = np.array([0.0, 0.5, 1.0, 1.5, 2.0, 3.0, 4.0, 6.0, -0.0, -0.5, -1.0, -1.5, -2.0, -3.0, -4.0, -6.0])


def pack_weight(w, fmt):
    k, n = w.shape
    w = f64(bf(w)).reshape(k // 32, 32, n)
    amax = np.abs(w).max(1)
    if fmt == "e4m3":
        byte = np.frexp(amax)[1] - 1 + 127 - 7
    else:
        mant, ex = np.frexp(amax / 6.0)
        byte = np.where(mant > 0.5, ex, ex - 1) + 127
    byte = np.clip(np.where(amax > 0, byte, 1), 1, 254)
    scaled = (w * np.exp2(127.0 - byte)[:, None, :]).reshape(k, n).astype(np.float32)
    by_word = np.ascontiguousarray(scaled.reshape(k // 512, 128, 4, n).transpose(0, 1, 3, 2))
    if fmt == "e4m3":
        words = by_word.astype(ml_dtypes.float8_e4m3fn).view(np.uint8)
    else:
        c = by_word.astype(ml_dtypes.float4_e2m1fn).view(np.uint8) & 0xF
        words = c[..., 0::2] | (c[..., 1::2] << 4)
    return np.ascontiguousarray(words), np.ascontiguousarray(byte.astype(np.uint8).reshape(k // 512, 16, n))


def unpack_weight(words, scales, fmt):
    g, p, n, _ = words.shape
    if fmt == "e4m3":
        vals = np.ascontiguousarray(words).view(ml_dtypes.float8_e4m3fn).astype(np.float64)
    else:
        nib = np.empty((g, p, n, 4), np.uint8)
        nib[..., 0::2] = words & 0xF
        nib[..., 1::2] = words >> 4
        vals = E2M1[nib]
    vals = vals * np.repeat(np.exp2(scales.astype(np.float64) - 127.0), 8, axis=1)[..., None]
    return vals.transpose(0, 1, 3, 2).reshape(g * 512, n)

def pack4(w):
    words, scales = pack_weight(w, "e2m1")
    return words.reshape(words.shape[0], 128, -1), scales


def unpack4(words, scales):
    return unpack_weight(words.reshape(words.shape[0], 128, -1, 2), scales, "e2m1")


B, N, K, D, L = 1, 1024, 16, 512, 512


def setup_inputs():
    s = mx_kscale(D)
    limit = np.sqrt(6.0 / (D + L))
    lone = np.random.random((B, N, 1)) < 0.125
    a = (0.3 + 0.7 * np.random.random((B, N, K + 1))) * np.where(lone, 0.4 / (K + 1), 1.0)
    targets = bf(np.random.standard_normal((B, N, D)) * s)
    neighbors = bf(np.random.standard_normal((B, N, K, D)) * s)
    words, scales = pack4(np.random.uniform(-limit, limit, (D, L)) / s[:, None])
    return {"targets": targets,
            "neighbors": neighbors,
            "a": bf(a),
            "kernel_words": words,
            "kernel_scales": scales}


def reference(targets, neighbors, a, kernel_words, kernel_scales):
    neighborhood = np.concatenate([f64(targets)[..., None, :], f64(neighbors)], axis=-2)
    y = (mxq(neighborhood, 3, "e4m3") @ unpack4(kernel_words, kernel_scales)).sum(axis=-2)
    factor = f64(a).sum(axis=-1, keepdims=True)
    factor = np.where(factor > 0.5, factor, np.ones_like(factor))
    y = y / factor
    return np.maximum(y, 0.0)

@@ -1,0 +1,212 @@
+from contextlib import ExitStack
+
+import concourse.mybir as mybir
+from concourse.masks import make_identity
+
+F32 = mybir.dt.float32
+BF16 = mybir.dt.bfloat16
+I32 = mybir.dt.int32
+U32 = mybir.dt.uint32
+U8 = mybir.dt.uint8
+FP8X4 = mybir.dt.float8_e4m3fn_x4
+FP4X4 = mybir.dt.float4_e2m1fn_x4
+ALU = mybir.AluOpType
+ACT = mybir.ActivationFunctionType
+
+P = 128
+NODES = 1024
+TILES = NODES // P
+NEIGHBOURS = 16
+MEMBERS = NEIGHBOURS + 1
+D = 512
+L = 512
+WORDS = D // 2
+MAX_BATCH = 9
+
+FLOPS = 2 * NODES * MEMBERS * D * L
+
+LOOKAHEAD = 2
+
+HEAD_BATCH_CUTS = {0: (2, 2, 4, 4, 5)}
+BATCH_CUTS = (8, 9)
+HEAD_LOAD_CUTS = {0: (2, 2, 4, 4, 5), 1: (8, 9), 2: (8, 9)}
+LOAD_CUTS = (17,)
+
+
+def cut_members(head, default):
+    pieces = []
+    for t in range(TILES):
+        m = 0
+        for c in head.get(t, default):
+            pieces.append((t, m, m + c))
+            m += c
+        assert m == MEMBERS
+    return pieces
+
+
+def quantise_widths(n):
+    widths = []
+    while n > 0:
+        w = 4 if n >= 4 else (2 if n >= 2 else 1)
+        widths.append(w)
+        n -= w
+    return widths
+
+
+def tile_singlegcnlayer_kernel(tc, targets, neighbors, a, kernel_words, kernel_scales, out):
+    nc = tc.nc
+    nb_view = neighbors[0].rearrange("(p t) m d -> t p m d", t=TILES)
+    tg_view = targets[0].rearrange("(p t) d -> t p d", t=TILES)
+    a_view = a[0].rearrange("(p t) k -> p t k", t=TILES)
+    out_view = out[0].rearrange("(p t) l -> t p l", t=TILES)
+
+    batches = cut_members(HEAD_BATCH_CUTS, BATCH_CUTS)
+    loads = cut_members(HEAD_LOAD_CUTS, LOAD_CUTS)
+    n_batches = len(batches)
+
+    with ExitStack() as ctx:
+        const = ctx.enter_context(tc.tile_pool(name="const", bufs=1))
+        xpool = ctx.enter_context(tc.tile_pool(name="xpool", bufs=1))
+        spool = ctx.enter_context(tc.tile_pool(name="spool", bufs=3))
+        gpool = ctx.enter_context(tc.tile_pool(name="gpool", bufs=3))
+        cpool = ctx.enter_context(tc.tile_pool(name="cpool", bufs=2))
+        opool = ctx.enter_context(tc.tile_pool(name="opool", bufs=4))
+        tpsum = ctx.enter_context(tc.psum_pool(name="tpsum", bufs=6))
+        apsum = ctx.enter_context(tc.psum_pool(name="apsum", bufs=2))
+        ctx.enter_context(tc.manual_schedule())
+
+        w_scales = const.tile([P, L], U8, align_bytes=64)
+        nc.vector.memset(w_scales[:].bitcast(I32), 0)
+        warm_in = const.tile([P, 1], F32)
+        warm_out = const.tile([P, 1], F32)
+        nc.vector.memset(warm_in[:], 0.0)
+        nc.scalar.activation(out=warm_out[:], in_=warm_in[:], func=ACT.Relu)
+        ident = const.tile([P, P], F32)
+        make_identity(nc, ident[:])
+        w_words = const.tile([P, 2 * L], U8, align_bytes=64)
+        a_sb = const.tile([P, TILES, MEMBERS], BF16)
+
+        x_sb = [xpool.tile([P, MEMBERS, D], BF16, name="x%d" % t) for t in range(TILES)]
+
+        def load_members(t, m0, m1):
+            hi = min(m1, NEIGHBOURS)
+            if m0 < hi:
+                nc.sync.dma_start(out=x_sb[t][:, m0:hi, :], in_=nb_view[t][:, m0:hi, :])
+            if m1 == MEMBERS:
+                nc.sync.dma_start(out=x_sb[t][:, NEIGHBOURS, :], in_=tg_view[t])
+
+        def load_weight():
+            nc.sync.dma_start(out=w_words[:].bitcast(I32), in_=kernel_words[0].bitcast(I32))
+            scale_rows = kernel_scales[0].bitcast(I32)
+            for r in range(4):
+                nc.sync.dma_start(out=w_scales[r:P:32, :].bitcast(I32), in_=scale_rows[r:16:4, :])
+
+        for i, (t, m0, m1) in enumerate(loads):
+            load_members(t, m0, m1)
+            if i == 1:
+                load_weight()
+            if (t, m1) == (0, MEMBERS):
+                nc.sync.dma_start(out=a_sb[:], in_=a_view)
+
+        xs_of = {}
+        g_of = {}
+        codes_of = {}
+        planes_of = {}
+        acc_of = {}
+        recip = const.tile([P, TILES], F32)
+
+        def sort_words(j):
+            t, m0, m1 = batches[j]
+            n = m1 - m0
+            xs = spool.tile([P, 2, MAX_BATCH, P], F32, tag="xs", name="xs")
+            xs_of[j] = xs
+            nc.vector.tensor_copy(
+                out=xs[:, :, 0:n, :],
+                in_=x_sb[t][:, m0:m1, :].bitcast(F32).rearrange("p m (j u) -> p u m j", u=2),
+            )
+
+        def transpose_and_drain(j):
+            t, m0, m1 = batches[j]
+            n = m1 - m0
+            xs = xs_of[j]
+            g = gpool.tile([P, MAX_BATCH * D], BF16, tag="g", name="g", align_bytes=64)
+            g_of[j] = g
+            g_words = g[:].bitcast(F32).rearrange("p (m r u) -> p m r u", r=P, u=2)
+            for q0 in range(0, n, 2):
+                width = min(2, n - q0)
+                pt = tpsum.tile([P, 2, 2, P], F32, tag="pt", name="pt")
+                for i in range(width):
+                    for u in range(2):
+                        nc.tensor.transpose(out=pt[:, i, u, :], in_=xs[:, u, q0 + i, :], identity=ident[:])
+                nc.scalar.copy(
+                    out=g_words[:, q0 : q0 + width, :, :],
+                    in_=pt[:, 0:width, :, :].rearrange("p i u r -> p i r u"),
+                )
+
+        def quantise(j):
+            t, m0, m1 = batches[j]
+            g = g_of[j]
+            codes = cpool.tile([P, MAX_BATCH * P], U32, tag="codes", name="codes", align_bytes=64)
+            planes = cpool.tile([P, MAX_BATCH * P], U8, tag="planes", name="planes", align_bytes=64)
+            codes_of[j] = codes
+            planes_of[j] = planes
+            m = 0
+            for w in quantise_widths(m1 - m0):
+                nc.vector.quantize_mx(
+                    out=codes[:, m * P : (m + w) * P].bitcast(FP8X4),
+                    scales=planes[:, m * P : (m + w) * P],
+                    in_=g[:, m * D : (m + w) * D],
+                )
+                m += w
+
+        def multiply(j):
+            t, m0, m1 = batches[j]
+            if m0 == 0:
+                acc_of[t] = apsum.tile([P, L], F32, tag="acc", name="acc")
+            acc = acc_of[t]
+            for m in range(m0, m1):
+                c = (m - m0) * P
+                nc.tensor.matmul_mx(
+                    out=acc[:],
+                    lhsT=codes_of[j][:, c : c + P].bitcast(FP8X4),
+                    lhsT_scale=planes_of[j][:, c : c + P],
+                    rhs=w_words[:].bitcast(FP4X4),
+                    rhs_scale=w_scales[:],
+                    start=(m == 0),
+                    stop=(m == MEMBERS - 1),
+                )
+
+        def factors():
+            total = const.tile([P, TILES], F32)
+            nc.vector.tensor_reduce(out=total[:], in_=a_sb[:], axis=mybir.AxisListType.X, op=ALU.add)
+            keep = const.tile([P, TILES], F32)
+            nc.vector.tensor_scalar(out=keep[:], in0=total[:], scalar1=0.5, scalar2=None, op0=ALU.is_gt)
+            kept = const.tile([P, TILES], F32)
+            nc.vector.tensor_tensor(out=kept[:], in0=total[:], in1=keep[:], op=ALU.mult)
+            ones = const.tile([P, TILES], F32)
+            nc.vector.tensor_scalar(out=ones[:], in0=total[:], scalar1=0.5, scalar2=None, op0=ALU.is_le)
+            factor = const.tile([P, TILES], F32)
+            nc.vector.tensor_tensor(out=factor[:], in0=kept[:], in1=ones[:], op=ALU.max)
+            nc.vector.reciprocal(out=recip[:], in_=factor[:])
+
+        def finish_tile(t):
+            o = opool.tile([P, L], F32, tag="o", name="o")
+            nc.scalar.activation(out=o[:], in_=acc_of[t][:], func=ACT.Relu, scale=recip[:, t : t + 1])
+            nc.sync.dma_start(out=out_view[t], in_=o[:])
+
+        def front(j):
+            sort_words(j)
+            transpose_and_drain(j)
+
+        for j in range(min(LOOKAHEAD, n_batches)):
+            front(j)
+        for j in range(n_batches):
+            if j + LOOKAHEAD < n_batches:
+                front(j + LOOKAHEAD)
+            quantise(j)
+            t, m0, m1 = batches[j]
+            if (t, m1) == (0, MEMBERS):
+                factors()
+            multiply(j)
+            if m1 == MEMBERS:
+                finish_tile(t)

@@ -20,28 +20,33 @@ NEIGHBOURS = 16
 MEMBERS = NEIGHBOURS + 1
 D = 512
 L = 512
-WORDS = D // 2
-MAX_BATCH = 9
+MAX_BATCH = 12
 
 FLOPS = 2 * NODES * MEMBERS * D * L
 
-LOOKAHEAD = 2
-
-HEAD_BATCH_CUTS = {0: (2, 2, 4, 4, 5)}
-BATCH_CUTS = (8, 9)
-HEAD_LOAD_CUTS = {0: (2, 2, 4, 4, 5), 1: (8, 9), 2: (8, 9)}
-LOAD_CUTS = (17,)
+BATCH_SIZES = (2, 2, 4, 6, 8, 10) + (12,) * 8 + (8,)
+LOAD_SIZES = (2, 2, 4, 6, 8, 10, 12, 12, 12, 17, 17, 17, 17)
 
 
-def cut_members(head, default):
+def cut_stream(sizes):
+    stream = [(t, m) for t in range(TILES) for m in range(MEMBERS)]
     pieces = []
-    for t in range(TILES):
-        m = 0
-        for c in head.get(t, default):
-            pieces.append((t, m, m + c))
-            m += c
-        assert m == MEMBERS
+    i = 0
+    for s in sizes:
+        pieces.append(stream[i : i + s])
+        i += s
+    assert i == len(stream)
     return pieces
+
+
+def runs_by_tile(piece):
+    runs = []
+    for i, (t, m) in enumerate(piece):
+        if runs and runs[-1][0] == t:
+            runs[-1] = (t, runs[-1][1], m + 1, runs[-1][3])
+        else:
+            runs.append((t, m, m + 1, i))
+    return runs
 
 
 def quantise_widths(n):
@@ -60,15 +65,15 @@ def tile_singlegcnlayer_kernel(tc, targets, neighbors, a, kernel_words, kernel_s
     a_view = a[0].rearrange("(p t) k -> p t k", t=TILES)
     out_view = out[0].rearrange("(p t) l -> t p l", t=TILES)
 
-    batches = cut_members(HEAD_BATCH_CUTS, BATCH_CUTS)
-    loads = cut_members(HEAD_LOAD_CUTS, LOAD_CUTS)
+    batches = cut_stream(BATCH_SIZES)
+    loads = cut_stream(LOAD_SIZES)
     n_batches = len(batches)
 
     with ExitStack() as ctx:
         const = ctx.enter_context(tc.tile_pool(name="const", bufs=1))
         xpool = ctx.enter_context(tc.tile_pool(name="xpool", bufs=1))
-        spool = ctx.enter_context(tc.tile_pool(name="spool", bufs=3))
-        gpool = ctx.enter_context(tc.tile_pool(name="gpool", bufs=3))
+        spool = ctx.enter_context(tc.tile_pool(name="spool", bufs=2))
+        gpool = ctx.enter_context(tc.tile_pool(name="gpool", bufs=2))
         cpool = ctx.enter_context(tc.tile_pool(name="cpool", bufs=2))
         opool = ctx.enter_context(tc.tile_pool(name="opool", bufs=4))
         tpsum = ctx.enter_context(tc.psum_pool(name="tpsum", bufs=6))
@@ -101,12 +106,13 @@ def tile_singlegcnlayer_kernel(tc, targets, neighbors, a, kernel_words, kernel_s
             for r in range(4):
                 nc.sync.dma_start(out=w_scales[r:P:32, :].bitcast(I32), in_=scale_rows[r:16:4, :])
 
-        for i, (t, m0, m1) in enumerate(loads):
-            load_members(t, m0, m1)
+        for i, piece in enumerate(loads):
+            for t, m0, m1, pos in runs_by_tile(piece):
+                load_members(t, m0, m1)
+                if (t, m1) == (0, MEMBERS):
+                    nc.sync.dma_start(out=a_sb[:], in_=a_view)
             if i == 1:
                 load_weight()
-            if (t, m1) == (0, MEMBERS):
-                nc.sync.dma_start(out=a_sb[:], in_=a_view)
 
         xs_of = {}
         g_of = {}
@@ -116,18 +122,16 @@ def tile_singlegcnlayer_kernel(tc, targets, neighbors, a, kernel_words, kernel_s
         recip = const.tile([P, TILES], F32)
 
         def sort_words(j):
-            t, m0, m1 = batches[j]
-            n = m1 - m0
             xs = spool.tile([P, 2, MAX_BATCH, P], F32, tag="xs", name="xs")
             xs_of[j] = xs
-            nc.vector.tensor_copy(
-                out=xs[:, :, 0:n, :],
-                in_=x_sb[t][:, m0:m1, :].bitcast(F32).rearrange("p m (j u) -> p u m j", u=2),
-            )
+            for t, m0, m1, pos in runs_by_tile(batches[j]):
+                nc.vector.tensor_copy(
+                    out=xs[:, :, pos : pos + m1 - m0, :],
+                    in_=x_sb[t][:, m0:m1, :].bitcast(F32).rearrange("p m (j u) -> p u m j", u=2),
+                )
 
         def transpose_and_drain(j):
-            t, m0, m1 = batches[j]
-            n = m1 - m0
+            n = len(batches[j])
             xs = xs_of[j]
             g = gpool.tile([P, MAX_BATCH * D], BF16, tag="g", name="g", align_bytes=64)
             g_of[j] = g
@@ -144,37 +148,19 @@ def tile_singlegcnlayer_kernel(tc, targets, neighbors, a, kernel_words, kernel_s
                 )
 
         def quantise(j):
-            t, m0, m1 = batches[j]
             g = g_of[j]
             codes = cpool.tile([P, MAX_BATCH * P], U32, tag="codes", name="codes", align_bytes=64)
             planes = cpool.tile([P, MAX_BATCH * P], U8, tag="planes", name="planes", align_bytes=64)
             codes_of[j] = codes
             planes_of[j] = planes
             m = 0
-            for w in quantise_widths(m1 - m0):
+            for w in quantise_widths(len(batches[j])):
                 nc.vector.quantize_mx(
                     out=codes[:, m * P : (m + w) * P].bitcast(FP8X4),
                     scales=planes[:, m * P : (m + w) * P],
                     in_=g[:, m * D : (m + w) * D],
                 )
                 m += w
-
-        def multiply(j):
-            t, m0, m1 = batches[j]
-            if m0 == 0:
-                acc_of[t] = apsum.tile([P, L], F32, tag="acc", name="acc")
-            acc = acc_of[t]
-            for m in range(m0, m1):
-                c = (m - m0) * P
-                nc.tensor.matmul_mx(
-                    out=acc[:],
-                    lhsT=codes_of[j][:, c : c + P].bitcast(FP8X4),
-                    lhsT_scale=planes_of[j][:, c : c + P],
-                    rhs=w_words[:].bitcast(FP4X4),
-                    rhs_scale=w_scales[:],
-                    start=(m == 0),
-                    stop=(m == MEMBERS - 1),
-                )
 
         def factors():
             total = const.tile([P, TILES], F32)
@@ -194,19 +180,31 @@ def tile_singlegcnlayer_kernel(tc, targets, neighbors, a, kernel_words, kernel_s
             nc.scalar.activation(out=o[:], in_=acc_of[t][:], func=ACT.Relu, scale=recip[:, t : t + 1])
             nc.sync.dma_start(out=out_view[t], in_=o[:])
 
+        def multiply(j):
+            for i, (t, m) in enumerate(batches[j]):
+                if m == 0:
+                    acc_of[t] = apsum.tile([P, L], F32, tag="acc", name="acc")
+                nc.tensor.matmul_mx(
+                    out=acc_of[t][:],
+                    lhsT=codes_of[j][:, i * P : (i + 1) * P].bitcast(FP8X4),
+                    lhsT_scale=planes_of[j][:, i * P : (i + 1) * P],
+                    rhs=w_words[:].bitcast(FP4X4),
+                    rhs_scale=w_scales[:],
+                    start=(m == 0),
+                    stop=(m == MEMBERS - 1),
+                )
+                if m == MEMBERS - 1:
+                    finish_tile(t)
+
         def front(j):
             sort_words(j)
             transpose_and_drain(j)
 
-        for j in range(min(LOOKAHEAD, n_batches)):
-            front(j)
+        front(0)
         for j in range(n_batches):
-            if j + LOOKAHEAD < n_batches:
-                front(j + LOOKAHEAD)
+            if j + 1 < n_batches:
+                front(j + 1)
             quantise(j)
-            t, m0, m1 = batches[j]
-            if (t, m1) == (0, MEMBERS):
+            if (0, MEMBERS - 1) in batches[j]:
                 factors()
             multiply(j)
-            if m1 == MEMBERS:
-                finish_tile(t)

@@ -20,12 +20,15 @@ NEIGHBOURS = 16
 MEMBERS = NEIGHBOURS + 1
 D = 512
 L = 512
-MAX_BATCH = 12
+CHUNK = 4
 
 FLOPS = 2 * NODES * MEMBERS * D * L
 
-BATCH_SIZES = (2, 2, 4, 6, 8, 10) + (12,) * 8 + (8,)
-LOAD_SIZES = (2, 2, 4, 6, 8, 10, 12, 12, 12, 17, 17, 17, 17)
+PHASE_SIZES = (2, 2, 4, 6, 8, 10, 14, 18, 18, 18, 18, 18)
+LOAD_SIZES = (2, 2, 4, 6, 8, 10, 14, 18, 4, 17, 17, 17, 17)
+XS_RING = 6
+G_RING = 3
+CODES_RING = 10
 
 
 def cut_stream(sizes):
@@ -49,15 +52,6 @@ def runs_by_tile(piece):
     return runs
 
 
-def quantise_widths(n):
-    widths = []
-    while n > 0:
-        w = 4 if n >= 4 else (2 if n >= 2 else 1)
-        widths.append(w)
-        n -= w
-    return widths
-
-
 def tile_singlegcnlayer_kernel(tc, targets, neighbors, a, kernel_words, kernel_scales, out):
     nc = tc.nc
     nb_view = neighbors[0].rearrange("(p t) m d -> t p m d", t=TILES)
@@ -65,16 +59,16 @@ def tile_singlegcnlayer_kernel(tc, targets, neighbors, a, kernel_words, kernel_s
     a_view = a[0].rearrange("(p t) k -> p t k", t=TILES)
     out_view = out[0].rearrange("(p t) l -> t p l", t=TILES)
 
-    batches = cut_stream(BATCH_SIZES)
+    phases = [[piece[i : i + CHUNK] for i in range(0, len(piece), CHUNK)] for piece in cut_stream(PHASE_SIZES)]
     loads = cut_stream(LOAD_SIZES)
-    n_batches = len(batches)
+    n_phases = len(phases)
 
     with ExitStack() as ctx:
         const = ctx.enter_context(tc.tile_pool(name="const", bufs=1))
         xpool = ctx.enter_context(tc.tile_pool(name="xpool", bufs=1))
-        spool = ctx.enter_context(tc.tile_pool(name="spool", bufs=2))
-        gpool = ctx.enter_context(tc.tile_pool(name="gpool", bufs=2))
-        cpool = ctx.enter_context(tc.tile_pool(name="cpool", bufs=2))
+        spool = ctx.enter_context(tc.tile_pool(name="spool", bufs=XS_RING))
+        gpool = ctx.enter_context(tc.tile_pool(name="gpool", bufs=G_RING))
+        cpool = ctx.enter_context(tc.tile_pool(name="cpool", bufs=CODES_RING))
         opool = ctx.enter_context(tc.tile_pool(name="opool", bufs=4))
         tpsum = ctx.enter_context(tc.psum_pool(name="tpsum", bufs=6))
         apsum = ctx.enter_context(tc.psum_pool(name="apsum", bufs=2))
@@ -121,46 +115,39 @@ def tile_singlegcnlayer_kernel(tc, targets, neighbors, a, kernel_words, kernel_s
         acc_of = {}
         recip = const.tile([P, TILES], F32)
 
-        def sort_words(j):
-            xs = spool.tile([P, 2, MAX_BATCH, P], F32, tag="xs", name="xs")
-            xs_of[j] = xs
-            for t, m0, m1, pos in runs_by_tile(batches[j]):
+        def sort_words(k, i):
+            xs = spool.tile([P, 2, CHUNK, P], F32, tag="xs", name="xs")
+            xs_of[(k, i)] = xs
+            for t, m0, m1, pos in runs_by_tile(phases[k][i]):
                 nc.vector.tensor_copy(
                     out=xs[:, :, pos : pos + m1 - m0, :],
                     in_=x_sb[t][:, m0:m1, :].bitcast(F32).rearrange("p m (j u) -> p u m j", u=2),
                 )
 
-        def transpose_and_drain(j):
-            n = len(batches[j])
-            xs = xs_of[j]
-            g = gpool.tile([P, MAX_BATCH * D], BF16, tag="g", name="g", align_bytes=64)
-            g_of[j] = g
+        def transpose_and_drain(k, i):
+            n = len(phases[k][i])
+            xs = xs_of[(k, i)]
+            g = gpool.tile([P, CHUNK * D], BF16, tag="g", name="g", align_bytes=64)
+            g_of[(k, i)] = g
             g_words = g[:].bitcast(F32).rearrange("p (m r u) -> p m r u", r=P, u=2)
             for q0 in range(0, n, 2):
-                width = min(2, n - q0)
                 pt = tpsum.tile([P, 2, 2, P], F32, tag="pt", name="pt")
-                for i in range(width):
+                for h in range(2):
                     for u in range(2):
-                        nc.tensor.transpose(out=pt[:, i, u, :], in_=xs[:, u, q0 + i, :], identity=ident[:])
-                nc.scalar.copy(
-                    out=g_words[:, q0 : q0 + width, :, :],
-                    in_=pt[:, 0:width, :, :].rearrange("p i u r -> p i r u"),
-                )
+                        nc.tensor.transpose(out=pt[:, h, u, :], in_=xs[:, u, q0 + h, :], identity=ident[:])
+                nc.scalar.copy(out=g_words[:, q0 : q0 + 2, :, :], in_=pt[:].rearrange("p h u r -> p h r u"))
 
-        def quantise(j):
-            g = g_of[j]
-            codes = cpool.tile([P, MAX_BATCH * P], U32, tag="codes", name="codes", align_bytes=64)
-            planes = cpool.tile([P, MAX_BATCH * P], U8, tag="planes", name="planes", align_bytes=64)
-            codes_of[j] = codes
-            planes_of[j] = planes
-            m = 0
-            for w in quantise_widths(len(batches[j])):
-                nc.vector.quantize_mx(
-                    out=codes[:, m * P : (m + w) * P].bitcast(FP8X4),
-                    scales=planes[:, m * P : (m + w) * P],
-                    in_=g[:, m * D : (m + w) * D],
-                )
-                m += w
+        def quantise(k, i):
+            n = len(phases[k][i])
+            codes = cpool.tile([P, CHUNK * P], U32, tag="codes", name="codes", align_bytes=64)
+            planes = cpool.tile([P, CHUNK * P], U8, tag="planes", name="planes", align_bytes=64)
+            codes_of[(k, i)] = codes
+            planes_of[(k, i)] = planes
+            nc.vector.quantize_mx(
+                out=codes[:, 0 : n * P].bitcast(FP8X4),
+                scales=planes[:, 0 : n * P],
+                in_=g_of[(k, i)][:, 0 : n * D],
+            )
 
         def factors():
             total = const.tile([P, TILES], F32)
@@ -180,31 +167,39 @@ def tile_singlegcnlayer_kernel(tc, targets, neighbors, a, kernel_words, kernel_s
             nc.scalar.activation(out=o[:], in_=acc_of[t][:], func=ACT.Relu, scale=recip[:, t : t + 1])
             nc.sync.dma_start(out=out_view[t], in_=o[:])
 
-        def multiply(j):
-            for i, (t, m) in enumerate(batches[j]):
-                if m == 0:
-                    acc_of[t] = apsum.tile([P, L], F32, tag="acc", name="acc")
-                nc.tensor.matmul_mx(
-                    out=acc_of[t][:],
-                    lhsT=codes_of[j][:, i * P : (i + 1) * P].bitcast(FP8X4),
-                    lhsT_scale=planes_of[j][:, i * P : (i + 1) * P],
-                    rhs=w_words[:].bitcast(FP4X4),
-                    rhs_scale=w_scales[:],
-                    start=(m == 0),
-                    stop=(m == MEMBERS - 1),
-                )
-                if m == MEMBERS - 1:
-                    finish_tile(t)
+        def multiply(k):
+            for i, chunk in enumerate(phases[k]):
+                for c, (t, m) in enumerate(chunk):
+                    if m == 0:
+                        acc_of[t] = apsum.tile([P, L], F32, tag="acc", name="acc")
+                    nc.tensor.matmul_mx(
+                        out=acc_of[t][:],
+                        lhsT=codes_of[(k, i)][:, c * P : (c + 1) * P].bitcast(FP8X4),
+                        lhsT_scale=planes_of[(k, i)][:, c * P : (c + 1) * P],
+                        rhs=w_words[:].bitcast(FP4X4),
+                        rhs_scale=w_scales[:],
+                        start=(m == 0),
+                        stop=(m == MEMBERS - 1),
+                    )
+                    if m == MEMBERS - 1:
+                        finish_tile(t)
 
-        def front(j):
-            sort_words(j)
-            transpose_and_drain(j)
-
-        front(0)
-        for j in range(n_batches):
-            if j + 1 < n_batches:
-                front(j + 1)
-            quantise(j)
-            if (0, MEMBERS - 1) in batches[j]:
+        for i in range(len(phases[0])):
+            sort_words(0, i)
+        for k in range(n_phases):
+            here = len(phases[k])
+            ahead = len(phases[k + 1]) if k + 1 < n_phases else 0
+            for i in range(here):
+                transpose_and_drain(k, i)
+                if i < ahead:
+                    sort_words(k + 1, i)
+                if i >= 1:
+                    quantise(k, i - 1)
+            for i in range(here, ahead):
+                sort_words(k + 1, i)
+            quantise(k, here - 1)
+            if k + 1 < n_phases and any((0, MEMBERS - 1) in chunk for chunk in phases[k + 1]):
                 factors()
-            multiply(j)
+            if k >= 1:
+                multiply(k - 1)
+        multiply(n_phases - 1)

@@ -20,15 +20,13 @@ NEIGHBOURS = 16
 MEMBERS = NEIGHBOURS + 1
 D = 512
 L = 512
-CHUNK = 4
+MAX_BATCH = 12
+SCALAR_SORTS = 3
 
 FLOPS = 2 * NODES * MEMBERS * D * L
 
-PHASE_SIZES = (2, 2, 4, 6, 8, 10, 14, 18, 18, 18, 18, 18)
-LOAD_SIZES = (2, 2, 4, 6, 8, 10, 14, 18, 4, 17, 17, 17, 17)
-XS_RING = 6
-G_RING = 3
-CODES_RING = 10
+BATCH_SIZES = (2, 2, 4, 6, 8, 10) + (12,) * 8 + (8,)
+LOAD_SIZES = (2, 2, 4, 6, 8, 10, 12, 12, 12, 17, 17, 17, 17)
 
 
 def cut_stream(sizes):
@@ -52,6 +50,15 @@ def runs_by_tile(piece):
     return runs
 
 
+def quantise_widths(n):
+    widths = []
+    while n > 0:
+        w = 8 if n >= 8 else (4 if n >= 4 else (2 if n >= 2 else 1))
+        widths.append(w)
+        n -= w
+    return widths
+
+
 def tile_singlegcnlayer_kernel(tc, targets, neighbors, a, kernel_words, kernel_scales, out):
     nc = tc.nc
     nb_view = neighbors[0].rearrange("(p t) m d -> t p m d", t=TILES)
@@ -59,16 +66,16 @@ def tile_singlegcnlayer_kernel(tc, targets, neighbors, a, kernel_words, kernel_s
     a_view = a[0].rearrange("(p t) k -> p t k", t=TILES)
     out_view = out[0].rearrange("(p t) l -> t p l", t=TILES)
 
-    phases = [[piece[i : i + CHUNK] for i in range(0, len(piece), CHUNK)] for piece in cut_stream(PHASE_SIZES)]
+    batches = cut_stream(BATCH_SIZES)
     loads = cut_stream(LOAD_SIZES)
-    n_phases = len(phases)
+    n_batches = len(batches)
 
     with ExitStack() as ctx:
         const = ctx.enter_context(tc.tile_pool(name="const", bufs=1))
         xpool = ctx.enter_context(tc.tile_pool(name="xpool", bufs=1))
-        spool = ctx.enter_context(tc.tile_pool(name="spool", bufs=XS_RING))
-        gpool = ctx.enter_context(tc.tile_pool(name="gpool", bufs=G_RING))
-        cpool = ctx.enter_context(tc.tile_pool(name="cpool", bufs=CODES_RING))
+        spool = ctx.enter_context(tc.tile_pool(name="spool", bufs=2))
+        gpool = ctx.enter_context(tc.tile_pool(name="gpool", bufs=2))
+        cpool = ctx.enter_context(tc.tile_pool(name="cpool", bufs=2))
         opool = ctx.enter_context(tc.tile_pool(name="opool", bufs=4))
         tpsum = ctx.enter_context(tc.psum_pool(name="tpsum", bufs=6))
         apsum = ctx.enter_context(tc.psum_pool(name="apsum", bufs=2))
@@ -115,39 +122,61 @@ def tile_singlegcnlayer_kernel(tc, targets, neighbors, a, kernel_words, kernel_s
         acc_of = {}
         recip = const.tile([P, TILES], F32)
 
-        def sort_words(k, i):
-            xs = spool.tile([P, 2, CHUNK, P], F32, tag="xs", name="xs")
-            xs_of[(k, i)] = xs
-            for t, m0, m1, pos in runs_by_tile(phases[k][i]):
-                nc.vector.tensor_copy(
-                    out=xs[:, :, pos : pos + m1 - m0, :],
+        def scalar_share(j):
+            return SCALAR_SORTS if len(batches[j]) == MAX_BATCH else 0
+
+        def sorted_tile(j):
+            if j not in xs_of:
+                xs_of[j] = spool.tile([P, 2, MAX_BATCH, P], F32, tag="xs", name="xs")
+            return xs_of[j]
+
+        def sort_words_scalar(j):
+            first = len(batches[j]) - scalar_share(j)
+            for t, m0, m1, pos in runs_by_tile(batches[j][first:]):
+                nc.scalar.copy(
+                    out=sorted_tile(j)[:, :, first + pos : first + pos + m1 - m0, :],
                     in_=x_sb[t][:, m0:m1, :].bitcast(F32).rearrange("p m (j u) -> p u m j", u=2),
                 )
 
-        def transpose_and_drain(k, i):
-            n = len(phases[k][i])
-            xs = xs_of[(k, i)]
-            g = gpool.tile([P, CHUNK * D], BF16, tag="g", name="g", align_bytes=64)
-            g_of[(k, i)] = g
+        def sort_words(j):
+            first = len(batches[j]) - scalar_share(j)
+            for t, m0, m1, pos in runs_by_tile(batches[j][:first]):
+                nc.vector.tensor_copy(
+                    out=sorted_tile(j)[:, :, pos : pos + m1 - m0, :],
+                    in_=x_sb[t][:, m0:m1, :].bitcast(F32).rearrange("p m (j u) -> p u m j", u=2),
+                )
+
+        def transpose_and_drain(j):
+            n = len(batches[j])
+            xs = xs_of[j]
+            g = gpool.tile([P, MAX_BATCH * D], BF16, tag="g", name="g", align_bytes=64)
+            g_of[j] = g
             g_words = g[:].bitcast(F32).rearrange("p (m r u) -> p m r u", r=P, u=2)
             for q0 in range(0, n, 2):
+                width = min(2, n - q0)
                 pt = tpsum.tile([P, 2, 2, P], F32, tag="pt", name="pt")
-                for h in range(2):
+                for i in range(width):
                     for u in range(2):
-                        nc.tensor.transpose(out=pt[:, h, u, :], in_=xs[:, u, q0 + h, :], identity=ident[:])
-                nc.scalar.copy(out=g_words[:, q0 : q0 + 2, :, :], in_=pt[:].rearrange("p h u r -> p h r u"))
+                        nc.tensor.transpose(out=pt[:, i, u, :], in_=xs[:, u, q0 + i, :], identity=ident[:])
+                nc.scalar.copy(
+                    out=g_words[:, q0 : q0 + width, :, :],
+                    in_=pt[:, 0:width, :, :].rearrange("p i u r -> p i r u"),
+                )
 
-        def quantise(k, i):
-            n = len(phases[k][i])
-            codes = cpool.tile([P, CHUNK * P], U32, tag="codes", name="codes", align_bytes=64)
-            planes = cpool.tile([P, CHUNK * P], U8, tag="planes", name="planes", align_bytes=64)
-            codes_of[(k, i)] = codes
-            planes_of[(k, i)] = planes
-            nc.vector.quantize_mx(
-                out=codes[:, 0 : n * P].bitcast(FP8X4),
-                scales=planes[:, 0 : n * P],
-                in_=g_of[(k, i)][:, 0 : n * D],
-            )
+        def quantise(j):
+            g = g_of[j]
+            codes = cpool.tile([P, MAX_BATCH * P], U32, tag="codes", name="codes", align_bytes=64)
+            planes = cpool.tile([P, MAX_BATCH * P], U8, tag="planes", name="planes", align_bytes=64)
+            codes_of[j] = codes
+            planes_of[j] = planes
+            m = 0
+            for w in quantise_widths(len(batches[j])):
+                nc.vector.quantize_mx(
+                    out=codes[:, m * P : (m + w) * P].bitcast(FP8X4),
+                    scales=planes[:, m * P : (m + w) * P],
+                    in_=g[:, m * D : (m + w) * D],
+                )
+                m += w
 
         def factors():
             total = const.tile([P, TILES], F32)
@@ -167,39 +196,33 @@ def tile_singlegcnlayer_kernel(tc, targets, neighbors, a, kernel_words, kernel_s
             nc.scalar.activation(out=o[:], in_=acc_of[t][:], func=ACT.Relu, scale=recip[:, t : t + 1])
             nc.sync.dma_start(out=out_view[t], in_=o[:])
 
-        def multiply(k):
-            for i, chunk in enumerate(phases[k]):
-                for c, (t, m) in enumerate(chunk):
-                    if m == 0:
-                        acc_of[t] = apsum.tile([P, L], F32, tag="acc", name="acc")
-                    nc.tensor.matmul_mx(
-                        out=acc_of[t][:],
-                        lhsT=codes_of[(k, i)][:, c * P : (c + 1) * P].bitcast(FP8X4),
-                        lhsT_scale=planes_of[(k, i)][:, c * P : (c + 1) * P],
-                        rhs=w_words[:].bitcast(FP4X4),
-                        rhs_scale=w_scales[:],
-                        start=(m == 0),
-                        stop=(m == MEMBERS - 1),
-                    )
-                    if m == MEMBERS - 1:
-                        finish_tile(t)
+        def multiply(j):
+            for i, (t, m) in enumerate(batches[j]):
+                if m == 0:
+                    acc_of[t] = apsum.tile([P, L], F32, tag="acc", name="acc")
+                nc.tensor.matmul_mx(
+                    out=acc_of[t][:],
+                    lhsT=codes_of[j][:, i * P : (i + 1) * P].bitcast(FP8X4),
+                    lhsT_scale=planes_of[j][:, i * P : (i + 1) * P],
+                    rhs=w_words[:].bitcast(FP4X4),
+                    rhs_scale=w_scales[:],
+                    start=(m == 0),
+                    stop=(m == MEMBERS - 1),
+                )
+                if m == MEMBERS - 1:
+                    finish_tile(t)
 
-        for i in range(len(phases[0])):
-            sort_words(0, i)
-        for k in range(n_phases):
-            here = len(phases[k])
-            ahead = len(phases[k + 1]) if k + 1 < n_phases else 0
-            for i in range(here):
-                transpose_and_drain(k, i)
-                if i < ahead:
-                    sort_words(k + 1, i)
-                if i >= 1:
-                    quantise(k, i - 1)
-            for i in range(here, ahead):
-                sort_words(k + 1, i)
-            quantise(k, here - 1)
-            if k + 1 < n_phases and any((0, MEMBERS - 1) in chunk for chunk in phases[k + 1]):
+        def front(j):
+            sort_words(j)
+            transpose_and_drain(j)
+
+        front(0)
+        for j in range(n_batches):
+            if j + 1 < n_batches:
+                front(j + 1)
+            if j + 2 < n_batches:
+                sort_words_scalar(j + 2)
+            quantise(j)
+            if (0, MEMBERS - 1) in batches[j]:
                 factors()
-            if k >= 1:
-                multiply(k - 1)
-        multiply(n_phases - 1)
+            multiply(j)

@@ -21,7 +21,9 @@ MEMBERS = NEIGHBOURS + 1
 D = 512
 L = 512
 MAX_BATCH = 12
-SCALAR_SORTS = 3
+WARM_START = 7
+WARM_BATCHES = 2
+WARM_AFTER = 2
 
 FLOPS = 2 * NODES * MEMBERS * D * L
 
@@ -53,7 +55,7 @@ def runs_by_tile(piece):
 def quantise_widths(n):
     widths = []
     while n > 0:
-        w = 8 if n >= 8 else (4 if n >= 4 else (2 if n >= 2 else 1))
+        w = 4 if n >= 4 else (2 if n >= 2 else 1)
         widths.append(w)
         n -= w
     return widths
@@ -81,12 +83,21 @@ def tile_singlegcnlayer_kernel(tc, targets, neighbors, a, kernel_words, kernel_s
         apsum = ctx.enter_context(tc.psum_pool(name="apsum", bufs=2))
         ctx.enter_context(tc.manual_schedule())
 
+        idle_rows = const.tile([P, L], BF16)
+        nc.vector.memset(idle_rows[:].bitcast(I32), 0)
         w_scales = const.tile([P, L], U8, align_bytes=64)
         nc.vector.memset(w_scales[:].bitcast(I32), 0)
         warm_in = const.tile([P, 1], F32)
         warm_out = const.tile([P, 1], F32)
         nc.vector.memset(warm_in[:], 0.0)
         nc.scalar.activation(out=warm_out[:], in_=warm_in[:], func=ACT.Relu)
+
+        def keep_clock(count):
+            scratch = tpsum.tile([P, L], F32, tag="pt", name="scratch")
+            for i in range(count):
+                nc.tensor.matmul(out=scratch[:], lhsT=idle_rows[:, 0:P], rhs=idle_rows[:], start=True, stop=True)
+
+        keep_clock(WARM_START)
         ident = const.tile([P, P], F32)
         make_identity(nc, ident[:])
         w_words = const.tile([P, 2 * L], U8, align_bytes=64)
@@ -122,27 +133,12 @@ def tile_singlegcnlayer_kernel(tc, targets, neighbors, a, kernel_words, kernel_s
         acc_of = {}
         recip = const.tile([P, TILES], F32)
 
-        def scalar_share(j):
-            return SCALAR_SORTS if len(batches[j]) == MAX_BATCH else 0
-
-        def sorted_tile(j):
-            if j not in xs_of:
-                xs_of[j] = spool.tile([P, 2, MAX_BATCH, P], F32, tag="xs", name="xs")
-            return xs_of[j]
-
-        def sort_words_scalar(j):
-            first = len(batches[j]) - scalar_share(j)
-            for t, m0, m1, pos in runs_by_tile(batches[j][first:]):
-                nc.scalar.copy(
-                    out=sorted_tile(j)[:, :, first + pos : first + pos + m1 - m0, :],
-                    in_=x_sb[t][:, m0:m1, :].bitcast(F32).rearrange("p m (j u) -> p u m j", u=2),
-                )
-
         def sort_words(j):
-            first = len(batches[j]) - scalar_share(j)
-            for t, m0, m1, pos in runs_by_tile(batches[j][:first]):
+            xs = spool.tile([P, 2, MAX_BATCH, P], F32, tag="xs", name="xs")
+            xs_of[j] = xs
+            for t, m0, m1, pos in runs_by_tile(batches[j]):
                 nc.vector.tensor_copy(
-                    out=sorted_tile(j)[:, :, pos : pos + m1 - m0, :],
+                    out=xs[:, :, pos : pos + m1 - m0, :],
                     in_=x_sb[t][:, m0:m1, :].bitcast(F32).rearrange("p m (j u) -> p u m j", u=2),
                 )
 
@@ -215,13 +211,13 @@ def tile_singlegcnlayer_kernel(tc, targets, neighbors, a, kernel_words, kernel_s
         def front(j):
             sort_words(j)
             transpose_and_drain(j)
+            if j < WARM_BATCHES:
+                keep_clock(WARM_AFTER)
 
         front(0)
         for j in range(n_batches):
             if j + 1 < n_batches:
                 front(j + 1)
-            if j + 2 < n_batches:
-                sort_words_scalar(j + 2)
             quantise(j)
             if (0, MEMBERS - 1) in batches[j]:
                 factors()

from contextlib import ExitStack

import concourse.mybir as mybir
from concourse.masks import make_identity

F32 = mybir.dt.float32
BF16 = mybir.dt.bfloat16
I32 = mybir.dt.int32
U32 = mybir.dt.uint32
U8 = mybir.dt.uint8
FP8X4 = mybir.dt.float8_e4m3fn_x4
FP4X4 = mybir.dt.float4_e2m1fn_x4
ALU = mybir.AluOpType
ACT = mybir.ActivationFunctionType

P = 128
NODES = 1024
TILES = NODES // P
NEIGHBOURS = 16
MEMBERS = NEIGHBOURS + 1
D = 512
L = 512
MAX_BATCH = 12
WARM_START = 7
WARM_BATCHES = 2
WARM_AFTER = 2

FLOPS = 2 * NODES * MEMBERS * D * L

BATCH_SIZES = (2, 2, 4, 6, 8, 10) + (12,) * 8 + (8,)
LOAD_SIZES = (2, 2, 4, 6, 8, 10, 12, 12, 12, 17, 17, 17, 17)


def cut_stream(sizes):
    stream = [(t, m) for t in range(TILES) for m in range(MEMBERS)]
    pieces = []
    i = 0
    for s in sizes:
        pieces.append(stream[i : i + s])
        i += s
    assert i == len(stream)
    return pieces


def runs_by_tile(piece):
    runs = []
    for i, (t, m) in enumerate(piece):
        if runs and runs[-1][0] == t:
            runs[-1] = (t, runs[-1][1], m + 1, runs[-1][3])
        else:
            runs.append((t, m, m + 1, i))
    return runs


def quantise_widths(n):
    widths = []
    while n > 0:
        w = 4 if n >= 4 else (2 if n >= 2 else 1)
        widths.append(w)
        n -= w
    return widths


def tile_singlegcnlayer_kernel(tc, targets, neighbors, a, kernel_words, kernel_scales, out):
    nc = tc.nc
    nb_view = neighbors[0].rearrange("(p t) m d -> t p m d", t=TILES)
    tg_view = targets[0].rearrange("(p t) d -> t p d", t=TILES)
    a_view = a[0].rearrange("(p t) k -> p t k", t=TILES)
    out_view = out[0].rearrange("(p t) l -> t p l", t=TILES)

    batches = cut_stream(BATCH_SIZES)
    loads = cut_stream(LOAD_SIZES)
    n_batches = len(batches)

    with ExitStack() as ctx:
        const = ctx.enter_context(tc.tile_pool(name="const", bufs=1))
        xpool = ctx.enter_context(tc.tile_pool(name="xpool", bufs=1))
        spool = ctx.enter_context(tc.tile_pool(name="spool", bufs=2))
        gpool = ctx.enter_context(tc.tile_pool(name="gpool", bufs=2))
        cpool = ctx.enter_context(tc.tile_pool(name="cpool", bufs=2))
        opool = ctx.enter_context(tc.tile_pool(name="opool", bufs=4))
        tpsum = ctx.enter_context(tc.psum_pool(name="tpsum", bufs=6))
        apsum = ctx.enter_context(tc.psum_pool(name="apsum", bufs=2))
        ctx.enter_context(tc.manual_schedule())

        idle_rows = const.tile([P, L], BF16)
        nc.vector.memset(idle_rows[:].bitcast(I32), 0)
        w_scales = const.tile([P, L], U8, align_bytes=64)
        nc.vector.memset(w_scales[:].bitcast(I32), 0)
        warm_in = const.tile([P, 1], F32)
        warm_out = const.tile([P, 1], F32)
        nc.vector.memset(warm_in[:], 0.0)
        nc.scalar.activation(out=warm_out[:], in_=warm_in[:], func=ACT.Relu)

        def keep_clock(count):
            scratch = tpsum.tile([P, L], F32, tag="pt", name="scratch")
            for i in range(count):
                nc.tensor.matmul(out=scratch[:], lhsT=idle_rows[:, 0:P], rhs=idle_rows[:], start=True, stop=True)

        keep_clock(WARM_START)
        ident = const.tile([P, P], F32)
        make_identity(nc, ident[:])
        w_words = const.tile([P, 2 * L], U8, align_bytes=64)
        a_sb = const.tile([P, TILES, MEMBERS], BF16)

        x_sb = [xpool.tile([P, MEMBERS, D], BF16, name="x%d" % t) for t in range(TILES)]

        def load_members(t, m0, m1):
            hi = min(m1, NEIGHBOURS)
            if m0 < hi:
                nc.sync.dma_start(out=x_sb[t][:, m0:hi, :], in_=nb_view[t][:, m0:hi, :])
            if m1 == MEMBERS:
                nc.sync.dma_start(out=x_sb[t][:, NEIGHBOURS, :], in_=tg_view[t])

        def load_weight():
            nc.sync.dma_start(out=w_words[:].bitcast(I32), in_=kernel_words[0].bitcast(I32))
            scale_rows = kernel_scales[0].bitcast(I32)
            for r in range(4):
                nc.sync.dma_start(out=w_scales[r:P:32, :].bitcast(I32), in_=scale_rows[r:16:4, :])

        for i, piece in enumerate(loads):
            for t, m0, m1, pos in runs_by_tile(piece):
                load_members(t, m0, m1)
                if (t, m1) == (0, MEMBERS):
                    nc.sync.dma_start(out=a_sb[:], in_=a_view)
            if i == 1:
                load_weight()

        xs_of = {}
        g_of = {}
        codes_of = {}
        planes_of = {}
        acc_of = {}
        recip = const.tile([P, TILES], F32)

        def sort_words(j):
            xs = spool.tile([P, 2, MAX_BATCH, P], F32, tag="xs", name="xs")
            xs_of[j] = xs
            for t, m0, m1, pos in runs_by_tile(batches[j]):
                nc.vector.tensor_copy(
                    out=xs[:, :, pos : pos + m1 - m0, :],
                    in_=x_sb[t][:, m0:m1, :].bitcast(F32).rearrange("p m (j u) -> p u m j", u=2),
                )

        def transpose_and_drain(j):
            n = len(batches[j])
            xs = xs_of[j]
            g = gpool.tile([P, MAX_BATCH * D], BF16, tag="g", name="g", align_bytes=64)
            g_of[j] = g
            g_words = g[:].bitcast(F32).rearrange("p (m r u) -> p m r u", r=P, u=2)
            for q0 in range(0, n, 2):
                width = min(2, n - q0)
                pt = tpsum.tile([P, 2, 2, P], F32, tag="pt", name="pt")
                for i in range(width):
                    for u in range(2):
                        nc.tensor.transpose(out=pt[:, i, u, :], in_=xs[:, u, q0 + i, :], identity=ident[:])
                nc.scalar.copy(
                    out=g_words[:, q0 : q0 + width, :, :],
                    in_=pt[:, 0:width, :, :].rearrange("p i u r -> p i r u"),
                )

        def quantise(j):
            g = g_of[j]
            codes = cpool.tile([P, MAX_BATCH * P], U32, tag="codes", name="codes", align_bytes=64)
            planes = cpool.tile([P, MAX_BATCH * P], U8, tag="planes", name="planes", align_bytes=64)
            codes_of[j] = codes
            planes_of[j] = planes
            m = 0
            for w in quantise_widths(len(batches[j])):
                nc.vector.quantize_mx(
                    out=codes[:, m * P : (m + w) * P].bitcast(FP8X4),
                    scales=planes[:, m * P : (m + w) * P],
                    in_=g[:, m * D : (m + w) * D],
                )
                m += w

        def factors():
            total = const.tile([P, TILES], F32)
            nc.vector.tensor_reduce(out=total[:], in_=a_sb[:], axis=mybir.AxisListType.X, op=ALU.add)
            keep = const.tile([P, TILES], F32)
            nc.vector.tensor_scalar(out=keep[:], in0=total[:], scalar1=0.5, scalar2=None, op0=ALU.is_gt)
            kept = const.tile([P, TILES], F32)
            nc.vector.tensor_tensor(out=kept[:], in0=total[:], in1=keep[:], op=ALU.mult)
            ones = const.tile([P, TILES], F32)
            nc.vector.tensor_scalar(out=ones[:], in0=total[:], scalar1=0.5, scalar2=None, op0=ALU.is_le)
            factor = const.tile([P, TILES], F32)
            nc.vector.tensor_tensor(out=factor[:], in0=kept[:], in1=ones[:], op=ALU.max)
            nc.vector.reciprocal(out=recip[:], in_=factor[:])

        def finish_tile(t):
            o = opool.tile([P, L], F32, tag="o", name="o")
            nc.scalar.activation(out=o[:], in_=acc_of[t][:], func=ACT.Relu, scale=recip[:, t : t + 1])
            nc.sync.dma_start(out=out_view[t], in_=o[:])

        def multiply(j):
            for i, (t, m) in enumerate(batches[j]):
                if m == 0:
                    acc_of[t] = apsum.tile([P, L], F32, tag="acc", name="acc")
                nc.tensor.matmul_mx(
                    out=acc_of[t][:],
                    lhsT=codes_of[j][:, i * P : (i + 1) * P].bitcast(FP8X4),
                    lhsT_scale=planes_of[j][:, i * P : (i + 1) * P],
                    rhs=w_words[:].bitcast(FP4X4),
                    rhs_scale=w_scales[:],
                    start=(m == 0),
                    stop=(m == MEMBERS - 1),
                )
                if m == MEMBERS - 1:
                    finish_tile(t)

        def front(j):
            sort_words(j)
            transpose_and_drain(j)
            if j < WARM_BATCHES:
                keep_clock(WARM_AFTER)

        front(0)
        for j in range(n_batches):
            if j + 1 < n_batches:
                front(j + 1)
            quantise(j)
            if (0, MEMBERS - 1) in batches[j]:
                factors()
            multiply(j)
